import numpy as np
import ml_dtypes


def mxq(x, axis, fmt="e4m3"):
    dtype, down = {"e4m3": (ml_dtypes.float8_e4m3fn, 7), "e5m2": (ml_dtypes.float8_e5m2, 14)}[fmt]
    v = np.moveaxis(np.asarray(x, np.float32).astype(ml_dtypes.bfloat16).astype(np.float64), axis, -1)
    blocks = v.reshape(v.shape[:-1] + (-1, 32))
    amax = np.abs(blocks).max(-1, keepdims=True)
    byte = np.maximum(np.where(amax > 0, np.frexp(amax)[1] - 1 + 127, 0) - down, 1)
    scale = np.exp2(byte - 127.0)
    codes = (blocks / scale).astype(np.float32).astype(dtype).astype(np.float64)
    return np.moveaxis((codes * scale).reshape(v.shape), -1, axis)


WIDE = False


def mx_kscale(k):
    if not WIDE:
        return np.ones(k)
    levels = np.array([10, -10, 5, -5, 0])
    if k % 512:
        return np.exp2(np.random.permutation(np.resize(levels, k // 32))).repeat(32)
    a = np.empty((k // 512, 16))
    for p in range(k // 512):
        a[p, :8] = np.random.permutation(np.resize(levels, 8))
        for g in range(8):
            far = levels[np.abs(levels - a[p, g]) >= 10]
            a[p, g + 8] = far[np.random.randint(len(far))]
    return np.exp2(a.ravel()).repeat(32)


BF16 = ml_dtypes.bfloat16


def bf(x):
    return np.asarray(x, np.float32).astype(BF16)


def f64(x):
    return np.asarray(x).astype(np.float64)


B, D, E, H, W, SHIFT = 4, 1024, 1024, 16, 16, 5
EPS = 1e-5


def erf(v):
    a = np.clip(v, -6.0, 6.0)
    a2 = 2.0 * a * a
    term = a.copy()
    tot = a.copy()
    for n in range(120):
        term = term * a2 / (2 * n + 3)
        tot = tot + term
    return 2.0 / np.sqrt(np.pi) * np.exp(-a * a) * tot


def gelu(v):
    return 0.5 * v * (1.0 + erf(v / np.sqrt(2.0)))


def conv1x1(x, w, b):
    n, c, hh, ww = x.shape
    y = mxq(w, 1, "e4m3") @ mxq(x.reshape(n, c, hh * ww), 1, "e4m3")
    return y.reshape(n, -1, hh, ww) + b[None, :, None, None]


def group_norm1(x, gamma, beta):
    m = x.mean(axis=(1, 2, 3), keepdims=True)
    v = x.var(axis=(1, 2, 3), keepdims=True)
    xh = (x - m) / np.sqrt(v + EPS)
    return xh * gamma[None, :, None, None] + beta[None, :, None, None]


def setup_inputs():
    s = mx_kscale(D)
    return {"x": bf(np.random.standard_normal((B, D, H, W)) * s[None, :, None, None]),
            "w1": bf(np.random.standard_normal((E, D)) / np.sqrt(D) / s[None, :]),
            "b1": bf(np.random.standard_normal(E) * 0.3),
            "g1": bf(1.0 + 0.1 * np.random.standard_normal(E)),
            "be1": bf(0.2 * np.random.standard_normal(E))}


def reference(x, w1, b1, g1, be1):
    y = conv1x1(f64(x), f64(w1), f64(b1))
    return gelu(group_norm1(y, f64(g1), f64(be1)))

@@ -1,0 +1,327 @@
+from contextlib import ExitStack
+
+import concourse.mybir as mybir
+from concourse.masks import make_identity
+
+F32 = mybir.dt.float32
+BF16 = mybir.dt.bfloat16
+U32 = mybir.dt.uint32
+U8 = mybir.dt.uint8
+FP8X4 = mybir.dt.float8_e4m3fn_x4
+ALU = mybir.AluOpType
+ACT = mybir.ActivationFunctionType
+AX = mybir.AxisListType
+
+FLOPS = 2 * 1024 * 1024 * 1024
+
+P = 128
+NS = 4
+NT = 8
+NB = 4
+PIX = 256
+EPS = 1e-5
+
+
+def tile_axialshift_pa_kernel(tc, x, w1, b1, g1, be1, out):
+    nc = tc.nc
+    with ExitStack() as ctx:
+        keep = ctx.enter_context(tc.tile_pool(name="keep", bufs=1))
+        psum = ctx.enter_context(tc.psum_pool(name="psum", bufs=1))
+        ctx.enter_context(tc.manual_schedule())
+
+        w_sb = keep.tile([P, NT, 1024], BF16)
+        x_sb = keep.tile([P, NS, 2, 4, PIX], BF16)
+        wg = keep.tile([P, NT, 2, P, 4], BF16, align_bytes=64)
+        xg = keep.tile([P, NS, 2, PIX, 4], BF16, align_bytes=64)
+        wc = keep.tile([P, NT, 2 * P], U32, align_bytes=64)
+        ws = keep.tile([P, NT, 2 * P], U8, align_bytes=64)
+        xc = keep.tile([P, NS, 2 * PIX], U32, align_bytes=64)
+        xs = keep.tile([P, NS, 2 * PIX], U8, align_bytes=64)
+        o_sb = keep.tile([P, NS, NT, PIX], F32)
+
+        ident = keep.tile([P, P], F32)
+        cmat = keep.tile([P, P], F32)
+        brhs = keep.tile([P, 4], F32)
+        mhalf = keep.tile([P, 1], F32)
+        junk_in = keep.tile([P, 1], F32)
+        junk_out = keep.tile([P, 1], F32)
+        b_bf = keep.tile([P, NT], BF16)
+        g_bf = keep.tile([P, NT], BF16)
+        be_bf = keep.tile([P, NT], BF16)
+        b32 = keep.tile([P, NT], F32)
+        nmb = keep.tile([P, 1], F32)
+        addc = keep.tile([P, NT, 2], F32)
+        stt = keep.tile([P, NS, NB, 6], F32)
+        rr = keep.tile([P, NS, 8], F32)
+        gu = keep.tile([P, NS, 2, NT], F32)
+        zb = keep.tile([P, 2, NT], F32)
+        sb = keep.tile([P, NS, 2, NT], F32)
+        ve = [keep.tile([P, 1], F32, name="ve%d" % n) for n in range(NS)]
+        rstd = [keep.tile([P, 1], F32, name="rstd%d" % n) for n in range(NS)]
+
+        w_view = w1.rearrange("(p t) k -> p t k", t=NT)
+        o_view = [out[n].rearrange("(p t) h w -> p t (h w)", t=NT) for n in range(NS)]
+        wt_tiles = {}
+        y_tiles = {}
+        ps_tiles = {}
+
+        def bank(k, shape, name):
+            return psum.tile(shape, F32, tag="bk%d" % k, name=name)
+
+        def params():
+            nc.scalar.dma_start(out=b_bf[:], in_=b1.rearrange("(p t) -> p t", t=NT))
+            nc.scalar.dma_start(out=g_bf[:], in_=g1.rearrange("(p t) -> p t", t=NT))
+            nc.scalar.dma_start(out=be_bf[:], in_=be1.rearrange("(p t) -> p t", t=NT))
+            nc.vector.memset(junk_in[:], 0.0)
+            nc.scalar.activation(out=junk_out[:], in_=junk_in[:], func=ACT.Gelu)
+            make_identity(nc, ident[:])
+            nc.vector.memset(cmat[:], 1.0 / P)
+            nc.vector.memset(addc[:], PIX * EPS)
+            nc.vector.memset(brhs[:], 0.0)
+            nc.vector.memset(mhalf[:], -0.5)
+            nc.vector.memset(rr[:], 0.0)
+            nc.vector.memset(rr[:, :, 1:2], -1.0)
+            nc.vector.memset(zb[:], 0.0)
+
+        def lw(t):
+            nc.sync.dma_start(out=w_sb[:, t, :], in_=w_view[:, t, :])
+
+        def lx(n):
+            nc.sync.dma_start(
+                out=x_sb[:, n].rearrange("p g s w -> p g (s w)"),
+                in_=x[n].rearrange("(g q s) h w -> q g (s h w)", g=2, q=P, s=4),
+            )
+
+        def cvt():
+            nc.vector.tensor_copy(out=b32[:], in_=b_bf[:])
+            nc.vector.tensor_copy(out=gu[:, :, 0, :],
+                                  in_=g_bf[:].unsqueeze(1).to_broadcast([P, NS, NT]))
+            nc.vector.tensor_copy(out=zb[:, 1, :], in_=be_bf[:])
+            nc.vector.tensor_reduce(out=brhs[:, 0:1], in_=b32[:], axis=AX.X, op=ALU.add)
+
+        def mmb(k):
+            psb = bank(k, [P, 4], "psb")
+            ps_tiles["b"] = psb
+            nc.tensor.matmul(psb[:], lhsT=cmat[:], rhs=brhs[:], start=True, stop=True)
+
+        def bp():
+            nc.vector.tensor_scalar(out=nmb[:], in0=ps_tiles["b"][:, 0:1], scalar1=-1.0 / NT,
+                                    scalar2=None, op0=ALU.mult)
+            nc.vector.tensor_scalar(out=addc[:, :, 0], in0=b32[:], scalar1=nmb[:], scalar2=None,
+                                    op0=ALU.add)
+
+        def wT(t, k):
+            wt = bank(k, [P, 4, P], "wt%d" % t)
+            wt_tiles[t] = wt
+            words = w_sb[:, t, :].bitcast(F32)
+            for a in range(4):
+                g, u = divmod(a, 2)
+                nc.tensor.transpose(wt[:, a, :], words[:, 256 * g + u:256 * (g + 1):2], ident[:])
+
+        def wC(t, eng="S"):
+            dst = wg[:, t].rearrange("p g o s -> p (g o s)").bitcast(F32)
+            dst = dst.rearrange("p (g o u) -> p g o u", g=2, u=2)
+            src = wt_tiles[t][:].rearrange("p (g u) o -> p g o u", g=2)
+            if eng == "S":
+                nc.scalar.copy(out=dst, in_=src)
+            else:
+                nc.vector.tensor_copy(out=dst, in_=src)
+
+        def wQ(t):
+            nc.vector.quantize_mx(
+                out=wc[:, t, :].bitcast(FP8X4),
+                scales=ws[:, t, :],
+                in_=wg[:, t].rearrange("p g o s -> p (g o s)"),
+            )
+
+        def xR(n, g, eng):
+            dst = xg[:, n, g].rearrange("p (c i) s -> p c s i", i=4)
+            src = x_sb[:, n, g].rearrange("p s (c i) -> p c s i", i=4)
+            if eng == "V":
+                nc.vector.tensor_copy(out=dst, in_=src)
+            elif eng == "S":
+                nc.scalar.copy(out=dst, in_=src)
+            else:
+                nc.gpsimd.tensor_scalar(out=dst, in0=src, scalar1=1.0, scalar2=0.0,
+                                        op0=ALU.mult, op1=ALU.add)
+
+        def xQ(n):
+            nc.vector.quantize_mx(
+                out=xc[:, n, :].bitcast(FP8X4),
+                scales=xs[:, n, :],
+                in_=xg[:, n].rearrange("p g w s -> p (g w s)"),
+            )
+
+        def mx(n, b, k):
+            yb = bank(k, [P, 2, PIX], "y%d_%d" % (n, b))
+            y_tiles[(n, b)] = yb
+            for h in range(2):
+                t = 2 * b + h
+                for g in range(2):
+                    nc.tensor.matmul_mx(
+                        out=yb[:, h, :],
+                        lhsT=wc[:, t, g * P:(g + 1) * P].bitcast(FP8X4),
+                        lhsT_scale=ws[:, t, g * P:(g + 1) * P],
+                        rhs=xc[:, n, g * PIX:(g + 1) * PIX].bitcast(FP8X4),
+                        rhs_scale=xs[:, n, g * PIX:(g + 1) * PIX],
+                        start=(g == 0),
+                        stop=(g == 1),
+                    )
+
+        def st(n, b):
+            nc.vector.bn_stats(out=stt[:, n, b, :],
+                               in_=y_tiles[(n, b)][:].rearrange("p h w -> p w h"))
+
+        def V123(n):
+            pairs = stt[:, n].rearrange("p b (h s) -> p (b h) s", s=3)[:, :, 1:3]
+            nc.vector.tensor_tensor(out=pairs, in0=pairs, in1=addc[:], op=ALU.add)
+            nc.vector.bn_aggr(out=rr[:, n, 2:4], in_=stt[:, n].rearrange("p b s -> p (b s)"))
+            nc.vector.scalar_tensor_tensor(
+                out=rr[:, n, 4:6], in0=rr[:, n, 1:3], scalar=rr[:, n, 2:3],
+                in1=rr[:, n, 0:4:3], op0=ALU.mult, op1=ALU.add)
+
+        def mmS(n, k):
+            ps = bank(k, [P, 4], "ps%d" % n)
+            ps_tiles[n] = ps
+            nc.tensor.matmul(ps[:], lhsT=cmat[:], rhs=rr[:, n, 2:6], start=True, stop=True)
+
+        def Vau(n):
+            ps = ps_tiles[n]
+            nc.vector.tensor_scalar(out=ve[n][:], in0=ps[:, 0:1], scalar1=ps[:, 2:3],
+                                    scalar2=ps[:, 3:4], op0=ALU.mult, op1=ALU.add)
+            nc.gpsimd.tensor_tensor(out=rstd[n][:], in0=ve[n][:], in1=mhalf[:], op=ALU.pow)
+            nc.vector.scalar_tensor_tensor(
+                out=gu[:, n, 1, :], in0=addc[:, :, 0], scalar=ps[:, 2:3], in1=gu[:, n, 0, :],
+                op0=ALU.add, op1=ALU.mult)
+
+        def Vs(n):
+            nc.vector.scalar_tensor_tensor(
+                out=sb[:, n].rearrange("p a t -> p (a t)"),
+                in0=gu[:, n].rearrange("p a t -> p (a t)"), scalar=rstd[n][:],
+                in1=zb[:].rearrange("p a t -> p (a t)"), op0=ALU.mult, op1=ALU.add)
+
+        def ge(n, b):
+            yb = y_tiles[(n, b)]
+            for h in range(2):
+                t = 2 * b + h
+                nc.scalar.activation(out=o_sb[:, n, t, :], in_=yb[:, h, :], func=ACT.Gelu,
+                                     scale=sb[:, n, 0, t:t + 1], bias=sb[:, n, 1, t:t + 1])
+            nc.sync.dma_start(out=o_view[n][:, 2 * b:2 * b + 2, :],
+                              in_=o_sb[:, n, 2 * b:2 * b + 2, :])
+
+        params()
+        lx(0)
+        lx(1)
+        lw(0)
+        lw(1)
+        lw(2)
+        lw(3)
+        lw(4)
+        lw(5)
+        lw(6)
+        lw(7)
+        lx(2)
+        lx(3)
+        xR(0, 0, "V")
+        xR(0, 1, "V")
+        xQ(0)
+        xR(1, 0, "V")
+        xR(1, 1, "V")
+        xQ(1)
+        cvt()
+        wT(0, 4)
+        wC(0)
+        wT(1, 5)
+        wC(1)
+        wT(2, 6)
+        wC(2)
+        wT(3, 7)
+        wC(3)
+        mmb(3)
+        wQ(0)
+        wQ(1)
+        wQ(2)
+        wQ(3)
+        bp()
+        wT(4, 4)
+        wC(4)
+        wT(5, 5)
+        wC(5)
+        wT(6, 6)
+        wC(6)
+        wT(7, 7)
+        wC(7)
+        wQ(4)
+        wQ(5)
+        wQ(6)
+        wQ(7)
+        xR(2, 0, "S")
+        xR(2, 1, "S")
+        xR(3, 0, "S")
+        xR(3, 1, "S")
+        mx(0, 0, 0)
+        mx(0, 1, 1)
+        mx(0, 2, 2)
+        mx(0, 3, 3)
+        st(0, 0)
+        st(0, 1)
+        st(0, 2)
+        st(0, 3)
+        mx(1, 0, 4)
+        V123(0)
+        mmS(0, 5)
+        xQ(2)
+        Vau(0)
+        mx(1, 2, 6)
+        mx(1, 3, 7)
+        mx(1, 1, 5)
+        st(1, 0)
+        st(1, 2)
+        Vs(0)
+        st(1, 3)
+        st(1, 1)
+        ge(0, 0)
+        mx(2, 0, 0)
+        ge(0, 1)
+        V123(1)
+        mmS(1, 1)
+        xQ(3)
+        Vau(1)
+        ge(0, 2)
+        mx(2, 2, 2)
+        ge(0, 3)
+        mx(2, 3, 3)
+        mx(2, 1, 1)
+        st(2, 0)
+        st(2, 2)
+        Vs(1)
+        st(2, 3)
+        st(2, 1)
+        ge(1, 0)
+        mx(3, 0, 4)
+        ge(1, 1)
+        V123(2)
+        mmS(2, 5)
+        st(3, 0)
+        Vau(2)
+        ge(1, 2)
+        mx(3, 2, 6)
+        ge(1, 3)
+        mx(3, 3, 7)
+        mx(3, 1, 5)
+        st(3, 2)
+        st(3, 3)
+        Vs(2)
+        st(3, 1)
+        ge(2, 0)
+        V123(3)
+        mmS(3, 0)
+        Vau(3)
+        Vs(3)
+        ge(2, 1)
+        ge(2, 2)
+        ge(2, 3)
+        ge(3, 0)
+        ge(3, 1)
+        ge(3, 2)
+        ge(3, 3)

@@ -38,6 +38,7 @@ def tile_axialshift_pa_kernel(tc, x, w1, b1, g1, be1, out):
         xc = keep.tile([P, NS, 2 * PIX], U32, align_bytes=64)
         xs = keep.tile([P, NS, 2 * PIX], U8, align_bytes=64)
         o_sb = keep.tile([P, NS, NT, PIX], F32)
+        y_sb = keep.tile([P, NS, NT, PIX], F32)
 
         ident = keep.tile([P, P], F32)
         cmat = keep.tile([P, P], F32)
@@ -45,6 +46,7 @@ def tile_axialshift_pa_kernel(tc, x, w1, b1, g1, be1, out):
         mhalf = keep.tile([P, 1], F32)
         junk_in = keep.tile([P, 1], F32)
         junk_out = keep.tile([P, 1], F32)
+        zeros = keep.tile([P, 512], BF16)
         b_bf = keep.tile([P, NT], BF16)
         g_bf = keep.tile([P, NT], BF16)
         be_bf = keep.tile([P, NT], BF16)
@@ -72,6 +74,7 @@ def tile_axialshift_pa_kernel(tc, x, w1, b1, g1, be1, out):
             nc.scalar.dma_start(out=b_bf[:], in_=b1.rearrange("(p t) -> p t", t=NT))
             nc.scalar.dma_start(out=g_bf[:], in_=g1.rearrange("(p t) -> p t", t=NT))
             nc.scalar.dma_start(out=be_bf[:], in_=be1.rearrange("(p t) -> p t", t=NT))
+            nc.vector.memset(zeros[:], 0.0)
             nc.vector.memset(junk_in[:], 0.0)
             nc.scalar.activation(out=junk_out[:], in_=junk_in[:], func=ACT.Gelu)
             make_identity(nc, ident[:])
@@ -83,14 +86,19 @@ def tile_axialshift_pa_kernel(tc, x, w1, b1, g1, be1, out):
             nc.vector.memset(rr[:, :, 1:2], -1.0)
             nc.vector.memset(zb[:], 0.0)
 
-        def lw(t):
-            nc.sync.dma_start(out=w_sb[:, t, :], in_=w_view[:, t, :])
+        def lw(t, m=1):
+            nc.sync.dma_start(out=w_sb[:, t:t + m, :], in_=w_view[:, t:t + m, :])
 
-        def lx(n):
+        def lx(n, g):
             nc.sync.dma_start(
-                out=x_sb[:, n].rearrange("p g s w -> p g (s w)"),
-                in_=x[n].rearrange("(g q s) h w -> q g (s h w)", g=2, q=P, s=4),
+                out=x_sb[:, n, g].rearrange("p s w -> p (s w)"),
+                in_=x[n, 512 * g:512 * (g + 1)].rearrange("(q s) h w -> q (s h w)", s=4),
             )
+
+        def warm(k, count):
+            wm = bank(k, [P, 512], "warm")
+            for i in range(count):
+                nc.tensor.matmul(wm[:], lhsT=zeros[:, 0:P], rhs=zeros[:], start=True, stop=True)
 
         def cvt():
             nc.vector.tensor_copy(out=b32[:], in_=b_bf[:])
@@ -137,6 +145,9 @@ def tile_axialshift_pa_kernel(tc, x, w1, b1, g1, be1, out):
         def xR(n, g, eng):
             dst = xg[:, n, g].rearrange("p (c i) s -> p c s i", i=4)
             src = x_sb[:, n, g].rearrange("p s (c i) -> p c s i", i=4)
+            if eng == "G":
+                dst = xg[:, n, g]
+                src = x_sb[:, n, g].rearrange("p s w -> p w s")
             if eng == "V":
                 nc.vector.tensor_copy(out=dst, in_=src)
             elif eng == "S":
@@ -172,13 +183,26 @@ def tile_axialshift_pa_kernel(tc, x, w1, b1, g1, be1, out):
             nc.vector.bn_stats(out=stt[:, n, b, :],
                                in_=y_tiles[(n, b)][:].rearrange("p h w -> p w h"))
 
-        def V123(n):
+        def cp(n, b):
+            nc.scalar.copy(out=y_sb[:, n, 2 * b:2 * b + 2, :], in_=y_tiles[(n, b)][:])
+            y_tiles[(n, b)] = y_sb[:, n, 2 * b:2 * b + 2, :]
+
+        def Va(n):
             pairs = stt[:, n].rearrange("p b (h s) -> p (b h) s", s=3)[:, :, 1:3]
             nc.vector.tensor_tensor(out=pairs, in0=pairs, in1=addc[:], op=ALU.add)
+
+        def Vb(n):
             nc.vector.bn_aggr(out=rr[:, n, 2:4], in_=stt[:, n].rearrange("p b s -> p (b s)"))
+
+        def Vc(n):
             nc.vector.scalar_tensor_tensor(
                 out=rr[:, n, 4:6], in0=rr[:, n, 1:3], scalar=rr[:, n, 2:3],
                 in1=rr[:, n, 0:4:3], op0=ALU.mult, op1=ALU.add)
+
+        def V123(n):
+            Va(n)
+            Vb(n)
+            Vc(n)
 
         def mmS(n, k):
             ps = bank(k, [P, 4], "ps%d" % n)
@@ -210,117 +234,132 @@ def tile_axialshift_pa_kernel(tc, x, w1, b1, g1, be1, out):
                               in_=o_sb[:, n, 2 * b:2 * b + 2, :])
 
         params()
-        lx(0)
-        lx(1)
-        lw(0)
-        lw(1)
-        lw(2)
-        lw(3)
-        lw(4)
-        lw(5)
-        lw(6)
-        lw(7)
-        lx(2)
-        lx(3)
+        lx(0, 0)
+        lx(0, 1)
+        lw(0, 2)
+        lw(2, 2)
+        lx(1, 0)
+        lx(1, 1)
+        lw(4, 2)
+        lw(6, 2)
+        lx(2, 0)
+        lx(2, 1)
+        lx(3, 0)
+        lx(3, 1)
+        warm(2, 4)
         xR(0, 0, "V")
         xR(0, 1, "V")
-        xQ(0)
-        xR(1, 0, "V")
-        xR(1, 1, "V")
-        xQ(1)
         cvt()
-        wT(0, 4)
+        xQ(0)
+        wT(0, 3)
         wC(0)
-        wT(1, 5)
+        wT(1, 7)
         wC(1)
-        wT(2, 6)
-        wC(2)
-        wT(3, 7)
-        wC(3)
-        mmb(3)
+        mmb(5)
+        warm(1, 1)
         wQ(0)
         wQ(1)
+        bp()
+        wT(2, 2)
+        wC(2)
+        wT(3, 6)
+        wC(3)
+        mx(0, 0, 0)
         wQ(2)
         wQ(3)
-        bp()
-        wT(4, 4)
+        st(0, 0)
+        xR(1, 0, "G")
+        xR(1, 1, "S")
+        wT(4, 3)
         wC(4)
-        wT(5, 5)
+        wT(5, 7)
         wC(5)
-        wT(6, 6)
+        mx(0, 1, 1)
+        xQ(1)
+        wQ(4)
+        wQ(5)
+        wT(6, 3)
         wC(6)
         wT(7, 7)
         wC(7)
-        wQ(4)
-        wQ(5)
+        st(0, 1)
+        mx(0, 2, 2)
+        mx(1, 0, 4)
         wQ(6)
         wQ(7)
-        xR(2, 0, "S")
-        xR(2, 1, "S")
-        xR(3, 0, "S")
-        xR(3, 1, "S")
-        mx(0, 0, 0)
-        mx(0, 1, 1)
-        mx(0, 2, 2)
-        mx(0, 3, 3)
-        st(0, 0)
-        st(0, 1)
         st(0, 2)
+        xR(2, 0, "G")
+        xR(2, 1, "G")
+        xR(3, 0, "G")
+        xR(3, 1, "G")
+        mx(0, 3, 3)
+        mx(1, 1, 5)
+        cp(0, 0)
+        cp(0, 1)
+        cp(0, 2)
+        st(1, 0)
         st(0, 3)
-        mx(1, 0, 4)
-        V123(0)
-        mmS(0, 5)
-        xQ(2)
-        Vau(0)
         mx(1, 2, 6)
         mx(1, 3, 7)
-        mx(1, 1, 5)
-        st(1, 0)
+        Va(0)
+        st(1, 1)
+        Vb(0)
+        Vc(0)
+        mmS(0, 0)
+        cp(0, 3)
+        cp(1, 0)
+        cp(1, 1)
+        xQ(2)
+        Vau(0)
+        mx(2, 1, 1)
+        mx(2, 2, 2)
+        mx(2, 3, 3)
+        mx(2, 0, 0)
         st(1, 2)
         Vs(0)
-        st(1, 3)
-        st(1, 1)
         ge(0, 0)
-        mx(2, 0, 0)
         ge(0, 1)
-        V123(1)
-        mmS(1, 1)
-        xQ(3)
-        Vau(1)
         ge(0, 2)
-        mx(2, 2, 2)
         ge(0, 3)
-        mx(2, 3, 3)
-        mx(2, 1, 1)
-        st(2, 0)
-        st(2, 2)
-        Vs(1)
-        st(2, 3)
+        st(1, 3)
         st(2, 1)
-        ge(1, 0)
+        Va(1)
+        xQ(3)
+        Vb(1)
+        Vc(1)
+        mmS(1, 4)
+        mx(3, 1, 5)
+        st(2, 2)
+        Vau(1)
         mx(3, 0, 4)
-        ge(1, 1)
-        V123(2)
-        mmS(2, 5)
-        st(3, 0)
-        Vau(2)
+        cp(2, 1)
+        st(2, 3)
+        Vs(1)
         ge(1, 2)
         mx(3, 2, 6)
         ge(1, 3)
         mx(3, 3, 7)
-        mx(3, 1, 5)
+        ge(1, 0)
+        ge(1, 1)
+        st(2, 0)
+        st(3, 1)
+        Va(2)
+        st(3, 0)
+        Vb(2)
+        Vc(2)
+        mmS(2, 1)
         st(3, 2)
+        Vau(2)
         st(3, 3)
         Vs(2)
-        st(3, 1)
-        ge(2, 0)
+        ge(2, 1)
         V123(3)
-        mmS(3, 0)
+        mmS(3, 1)
         Vau(3)
         Vs(3)
-        ge(2, 1)
         ge(2, 2)
         ge(2, 3)
+        ge(2, 0)
         ge(3, 0)
         ge(3, 1)
         ge(3, 2)

@@ -268,7 +268,7 @@ def tile_axialshift_pa_kernel(tc, x, w1, b1, g1, be1, out):
         wQ(2)
         wQ(3)
         st(0, 0)
-        xR(1, 0, "G")
+        xR(1, 0, "V")
         xR(1, 1, "S")
         wT(4, 3)
         wC(4)
@@ -288,10 +288,8 @@ def tile_axialshift_pa_kernel(tc, x, w1, b1, g1, be1, out):
         wQ(6)
         wQ(7)
         st(0, 2)
-        xR(2, 0, "G")
-        xR(2, 1, "G")
-        xR(3, 0, "G")
-        xR(3, 1, "G")
+        xR(2, 0, "S")
+        xR(2, 1, "S")
         mx(0, 3, 3)
         mx(1, 1, 5)
         cp(0, 0)
@@ -308,7 +306,6 @@ def tile_axialshift_pa_kernel(tc, x, w1, b1, g1, be1, out):
         mmS(0, 0)
         cp(0, 3)
         cp(1, 0)
-        cp(1, 1)
         xQ(2)
         Vau(0)
         mx(2, 1, 1)
@@ -324,14 +321,17 @@ def tile_axialshift_pa_kernel(tc, x, w1, b1, g1, be1, out):
         st(1, 3)
         st(2, 1)
         Va(1)
-        xQ(3)
+        xR(3, 0, "V")
         Vb(1)
+        xR(3, 1, "V")
         Vc(1)
         mmS(1, 4)
-        mx(3, 1, 5)
-        st(2, 2)
+        xQ(3)
         Vau(1)
         mx(3, 0, 4)
+        st(2, 2)
+        cp(1, 1)
+        mx(3, 1, 5)
         cp(2, 1)
         st(2, 3)
         Vs(1)

@@ -235,131 +235,135 @@ def tile_axialshift_pa_kernel(tc, x, w1, b1, g1, be1, out):
 
         params()
         lx(0, 0)
-        lx(0, 1)
         lw(0, 2)
+        lx(0, 1)
         lw(2, 2)
         lx(1, 0)
-        lx(1, 1)
         lw(4, 2)
+        lx(1, 1)
         lw(6, 2)
         lx(2, 0)
         lx(2, 1)
         lx(3, 0)
         lx(3, 1)
-        warm(2, 4)
+        warm(7, 3)
+        cvt()
+        wT(0, 4)
+        wC(0)
+        wT(1, 5)
+        wC(1)
+        mmb(7)
         xR(0, 0, "V")
         xR(0, 1, "V")
-        cvt()
+        warm(1, 2)
         xQ(0)
-        wT(0, 3)
-        wC(0)
-        wT(1, 7)
-        wC(1)
-        mmb(5)
-        warm(1, 1)
         wQ(0)
-        wQ(1)
         bp()
-        wT(2, 2)
+        wT(2, 6)
         wC(2)
-        wT(3, 6)
+        wT(3, 3)
         wC(3)
-        mx(0, 0, 0)
-        wQ(2)
-        wQ(3)
-        st(0, 0)
+        wQ(1)
         xR(1, 0, "V")
-        xR(1, 1, "S")
-        wT(4, 3)
+        wQ(2)
+        mx(0, 0, 0)
+        wQ(3)
+        wT(4, 4)
         wC(4)
-        wT(5, 7)
+        wT(5, 5)
         wC(5)
+        st(0, 0)
         mx(0, 1, 1)
-        xQ(1)
+        xR(1, 1, "V")
         wQ(4)
         wQ(5)
-        wT(6, 3)
+        wT(6, 6)
         wC(6)
         wT(7, 7)
         wC(7)
         st(0, 1)
         mx(0, 2, 2)
+        xQ(1)
         mx(1, 0, 4)
         wQ(6)
         wQ(7)
         st(0, 2)
-        xR(2, 0, "S")
-        xR(2, 1, "S")
         mx(0, 3, 3)
         mx(1, 1, 5)
+        st(1, 0)
+        mx(1, 2, 6)
+        st(0, 3)
         cp(0, 0)
         cp(0, 1)
-        cp(0, 2)
-        st(1, 0)
-        st(0, 3)
-        mx(1, 2, 6)
+        xR(2, 0, "S")
+        xR(2, 1, "S")
         mx(1, 3, 7)
+        xQ(2)
         Va(0)
         st(1, 1)
         Vb(0)
-        Vc(0)
-        mmS(0, 0)
+        st(1, 2)
+        cp(0, 2)
         cp(0, 3)
-        cp(1, 0)
-        xQ(2)
-        Vau(0)
+        Vc(0)
+        st(1, 3)
         mx(2, 1, 1)
         mx(2, 2, 2)
+        mmS(0, 0)
+        cp(1, 0)
+        cp(1, 1)
+        st(2, 1)
+        Va(1)
+        Vau(0)
+        xR(3, 0, "S")
+        xR(3, 1, "S")
         mx(2, 3, 3)
         mx(2, 0, 0)
-        st(1, 2)
+        Vb(1)
+        st(2, 2)
+        Vc(1)
         Vs(0)
+        mmS(1, 4)
+        warm(5, 2)
+        cp(1, 2)
+        cp(2, 1)
         ge(0, 0)
         ge(0, 1)
         ge(0, 2)
         ge(0, 3)
-        st(1, 3)
-        st(2, 1)
-        Va(1)
-        xR(3, 0, "V")
-        Vb(1)
-        xR(3, 1, "V")
-        Vc(1)
-        mmS(1, 4)
-        xQ(3)
-        Vau(1)
-        mx(3, 0, 4)
-        st(2, 2)
-        cp(1, 1)
-        mx(3, 1, 5)
-        cp(2, 1)
         st(2, 3)
+        Vau(1)
+        xQ(3)
+        mx(3, 1, 5)
+        mx(3, 0, 4)
+        st(2, 0)
         Vs(1)
-        ge(1, 2)
         mx(3, 2, 6)
         ge(1, 3)
-        mx(3, 3, 7)
         ge(1, 0)
         ge(1, 1)
-        st(2, 0)
-        st(3, 1)
+        ge(1, 2)
         Va(2)
-        st(3, 0)
+        st(3, 1)
         Vb(2)
+        st(3, 0)
         Vc(2)
         mmS(2, 1)
+        mx(3, 3, 7)
         st(3, 2)
         Vau(2)
         st(3, 3)
         Vs(2)
+        Va(3)
         ge(2, 1)
-        V123(3)
-        mmS(3, 1)
-        Vau(3)
-        Vs(3)
         ge(2, 2)
         ge(2, 3)
         ge(2, 0)
+        Vb(3)
+        Vc(3)
+        mmS(3, 1)
+        Vau(3)
+        Vs(3)
         ge(3, 0)
         ge(3, 1)
         ge(3, 2)

@@ -135,26 +135,26 @@ def tile_axialshift_pa_kernel(tc, x, w1, b1, g1, be1, out):
             else:
                 nc.vector.tensor_copy(out=dst, in_=src)
 
-        def wQ(t):
+        def wQ(t, m=1):
             nc.vector.quantize_mx(
-                out=wc[:, t, :].bitcast(FP8X4),
-                scales=ws[:, t, :],
-                in_=wg[:, t].rearrange("p g o s -> p (g o s)"),
+                out=wc[:, t:t + m, :].rearrange("p t c -> p (t c)").bitcast(FP8X4),
+                scales=ws[:, t:t + m, :].rearrange("p t c -> p (t c)"),
+                in_=wg[:, t:t + m].rearrange("p t g o s -> p (t g o s)"),
             )
 
         def xR(n, g, eng):
             dst = xg[:, n, g].rearrange("p (c i) s -> p c s i", i=4)
             src = x_sb[:, n, g].rearrange("p s (c i) -> p c s i", i=4)
-            if eng == "G":
-                dst = xg[:, n, g]
-                src = x_sb[:, n, g].rearrange("p s w -> p w s")
             if eng == "V":
                 nc.vector.tensor_copy(out=dst, in_=src)
             elif eng == "S":
                 nc.scalar.copy(out=dst, in_=src)
             else:
-                nc.gpsimd.tensor_scalar(out=dst, in0=src, scalar1=1.0, scalar2=0.0,
-                                        op0=ALU.mult, op1=ALU.add)
+                for c in range(0, PIX, 64):
+                    nc.gpsimd.tensor_scalar(
+                        out=xg[:, n, g, c:c + 64, :],
+                        in0=x_sb[:, n, g, :, c:c + 64].rearrange("p s w -> p w s"),
+                        scalar1=1.0, scalar2=0.0, op0=ALU.mult, op1=ALU.add)
 
         def xQ(n):
             nc.vector.quantize_mx(
@@ -224,19 +224,23 @@ def tile_axialshift_pa_kernel(tc, x, w1, b1, g1, be1, out):
                 in0=gu[:, n].rearrange("p a t -> p (a t)"), scalar=rstd[n][:],
                 in1=zb[:].rearrange("p a t -> p (a t)"), op0=ALU.mult, op1=ALU.add)
 
-        def ge(n, b):
+        def ge(n, b, last=False):
             yb = y_tiles[(n, b)]
             for h in range(2):
                 t = 2 * b + h
                 nc.scalar.activation(out=o_sb[:, n, t, :], in_=yb[:, h, :], func=ACT.Gelu,
                                      scale=sb[:, n, 0, t:t + 1], bias=sb[:, n, 1, t:t + 1])
-            nc.sync.dma_start(out=o_view[n][:, 2 * b:2 * b + 2, :],
-                              in_=o_sb[:, n, 2 * b:2 * b + 2, :])
+                if last:
+                    nc.sync.dma_start(out=o_view[n][:, t:t + 1, :], in_=o_sb[:, n, t:t + 1, :])
+            if not last:
+                nc.sync.dma_start(out=o_view[n][:, 2 * b:2 * b + 2, :],
+                                  in_=o_sb[:, n, 2 * b:2 * b + 2, :])
 
         params()
         lx(0, 0)
-        lw(0, 2)
+        lw(0)
         lx(0, 1)
+        lw(1)
         lw(2, 2)
         lx(1, 0)
         lw(4, 2)
@@ -247,36 +251,33 @@ def tile_axialshift_pa_kernel(tc, x, w1, b1, g1, be1, out):
         lx(3, 0)
         lx(3, 1)
         warm(7, 3)
-        cvt()
         wT(0, 4)
         wC(0)
         wT(1, 5)
         wC(1)
-        mmb(7)
         xR(0, 0, "V")
         xR(0, 1, "V")
+        cvt()
         warm(1, 2)
         xQ(0)
-        wQ(0)
-        bp()
+        wQ(0, 2)
         wT(2, 6)
         wC(2)
         wT(3, 3)
         wC(3)
-        wQ(1)
         xR(1, 0, "V")
-        wQ(2)
+        mmb(7)
         mx(0, 0, 0)
-        wQ(3)
+        wQ(2, 2)
+        bp()
         wT(4, 4)
         wC(4)
         wT(5, 5)
         wC(5)
         st(0, 0)
         mx(0, 1, 1)
-        xR(1, 1, "V")
-        wQ(4)
-        wQ(5)
+        wQ(4, 2)
+        xR(1, 1, "S")
         wT(6, 6)
         wC(6)
         wT(7, 7)
@@ -285,59 +286,57 @@ def tile_axialshift_pa_kernel(tc, x, w1, b1, g1, be1, out):
         mx(0, 2, 2)
         xQ(1)
         mx(1, 0, 4)
-        wQ(6)
-        wQ(7)
-        st(0, 2)
-        mx(0, 3, 3)
         mx(1, 1, 5)
-        st(1, 0)
+        st(0, 2)
+        wQ(6, 2)
+        mx(0, 3, 3)
         mx(1, 2, 6)
+        mx(1, 3, 7)
+        st(1, 0)
+        st(1, 1)
         st(0, 3)
-        cp(0, 0)
-        cp(0, 1)
         xR(2, 0, "S")
         xR(2, 1, "S")
-        mx(1, 3, 7)
-        xQ(2)
-        Va(0)
-        st(1, 1)
-        Vb(0)
-        st(1, 2)
+        cp(0, 0)
+        cp(0, 1)
+        xR(3, 0, "S")
         cp(0, 2)
         cp(0, 3)
-        Vc(0)
+        xQ(2)
+        Va(0)
+        st(1, 2)
+        Vb(0)
         st(1, 3)
+        Vc(0)
         mx(2, 1, 1)
-        mx(2, 2, 2)
         mmS(0, 0)
         cp(1, 0)
-        cp(1, 1)
         st(2, 1)
         Va(1)
         Vau(0)
-        xR(3, 0, "S")
-        xR(3, 1, "S")
-        mx(2, 3, 3)
         mx(2, 0, 0)
         Vb(1)
-        st(2, 2)
-        Vc(1)
+        xR(3, 1, "V")
         Vs(0)
+        Vc(1)
         mmS(1, 4)
-        warm(5, 2)
+        mx(2, 2, 2)
+        mx(2, 3, 3)
+        cp(1, 1)
         cp(1, 2)
         cp(2, 1)
         ge(0, 0)
         ge(0, 1)
         ge(0, 2)
         ge(0, 3)
-        st(2, 3)
+        st(2, 0)
         Vau(1)
         xQ(3)
         mx(3, 1, 5)
         mx(3, 0, 4)
-        st(2, 0)
+        st(2, 2)
         Vs(1)
+        st(2, 3)
         mx(3, 2, 6)
         ge(1, 3)
         ge(1, 0)

@@ -284,6 +284,7 @@ def tile_axialshift_pa_kernel(tc, x, w1, b1, g1, be1, out):
         wC(7)
         st(0, 1)
         mx(0, 2, 2)
+        warm(3, 1)
         xQ(1)
         mx(1, 0, 4)
         mx(1, 1, 5)
@@ -310,6 +311,7 @@ def tile_axialshift_pa_kernel(tc, x, w1, b1, g1, be1, out):
         Vc(0)
         mx(2, 1, 1)
         mmS(0, 0)
+        warm(2, 2)
         cp(1, 0)
         st(2, 1)
         Va(1)
@@ -347,6 +349,7 @@ def tile_axialshift_pa_kernel(tc, x, w1, b1, g1, be1, out):
         Vb(2)
         st(3, 0)
         Vc(2)
+        warm(1, 2)
         mmS(2, 1)
         mx(3, 3, 7)
         st(3, 2)

@@ -191,6 +191,10 @@ def tile_axialshift_pa_kernel(tc, x, w1, b1, g1, be1, out):
             pairs = stt[:, n].rearrange("p b (h s) -> p (b h) s", s=3)[:, :, 1:3]
             nc.vector.tensor_tensor(out=pairs, in0=pairs, in1=addc[:], op=ALU.add)
 
+        def Ga(n):
+            pairs = stt[:, n].rearrange("p b (h s) -> p (b h) s", s=3)[:, :, 1:3]
+            nc.gpsimd.tensor_tensor(out=pairs, in0=pairs, in1=addc[:], op=ALU.add)
+
         def Vb(n):
             nc.vector.bn_aggr(out=rr[:, n, 2:4], in_=stt[:, n].rearrange("p b s -> p (b s)"))
 
@@ -238,134 +242,130 @@ def tile_axialshift_pa_kernel(tc, x, w1, b1, g1, be1, out):
 
         params()
         lx(0, 0)
-        lw(0)
         lx(0, 1)
+        lw(0)
         lw(1)
-        lw(2, 2)
         lx(1, 0)
-        lw(4, 2)
         lx(1, 1)
+        lw(2, 2)
+        lw(4, 2)
         lw(6, 2)
         lx(2, 0)
         lx(2, 1)
         lx(3, 0)
         lx(3, 1)
         warm(7, 3)
+        xR(0, 0, "V")
+        xR(0, 1, "V")
         wT(0, 4)
         wC(0)
         wT(1, 5)
         wC(1)
-        xR(0, 0, "V")
-        xR(0, 1, "V")
         cvt()
-        warm(1, 2)
+        warm(1, 4)
         xQ(0)
+        xR(1, 0, "V")
+        xR(1, 1, "S")
         wQ(0, 2)
+        mmb(7)
         wT(2, 6)
         wC(2)
         wT(3, 3)
         wC(3)
-        xR(1, 0, "V")
-        mmb(7)
         mx(0, 0, 0)
-        wQ(2, 2)
         bp()
-        wT(4, 4)
+        xQ(1)
+        wT(4, 7)
         wC(4)
         wT(5, 5)
         wC(5)
         st(0, 0)
-        mx(0, 1, 1)
-        wQ(4, 2)
-        xR(1, 1, "S")
+        wQ(2, 2)
         wT(6, 6)
         wC(6)
-        wT(7, 7)
+        wT(7, 3)
         wC(7)
+        mx(0, 1, 2)
+        mx(1, 0, 1)
+        wQ(4, 2)
+        mx(1, 1, 4)
         st(0, 1)
-        mx(0, 2, 2)
-        warm(3, 1)
-        xQ(1)
-        mx(1, 0, 4)
-        mx(1, 1, 5)
-        st(0, 2)
+        mx(0, 2, 7)
         wQ(6, 2)
-        mx(0, 3, 3)
-        mx(1, 2, 6)
-        mx(1, 3, 7)
         st(1, 0)
-        st(1, 1)
-        st(0, 3)
+        mx(0, 3, 3)
+        mx(1, 2, 5)
+        mx(1, 3, 6)
+        st(0, 2)
         xR(2, 0, "S")
         xR(2, 1, "S")
         cp(0, 0)
+        cp(1, 0)
+        st(1, 1)
+        st(0, 3)
         cp(0, 1)
-        xR(3, 0, "S")
         cp(0, 2)
-        cp(0, 3)
         xQ(2)
-        Va(0)
+        Ga(0)
         st(1, 2)
         Vb(0)
+        mx(2, 0, 1)
+        mx(2, 1, 2)
         st(1, 3)
         Vc(0)
-        mx(2, 1, 1)
         mmS(0, 0)
-        warm(2, 2)
-        cp(1, 0)
-        st(2, 1)
-        Va(1)
-        Vau(0)
-        mx(2, 0, 0)
-        Vb(1)
-        xR(3, 1, "V")
-        Vs(0)
-        Vc(1)
-        mmS(1, 4)
-        mx(2, 2, 2)
-        mx(2, 3, 3)
         cp(1, 1)
-        cp(1, 2)
-        cp(2, 1)
+        Ga(1)
+        st(2, 0)
+        Vau(0)
+        Vb(1)
+        mx(2, 2, 7)
+        xR(3, 0, "S")
+        st(2, 1)
+        Vc(1)
+        mx(2, 3, 4)
+        mmS(1, 0)
+        xR(3, 1, "S")
+        Vs(0)
+        ge(0, 3)
         ge(0, 0)
+        st(2, 2)
+        Vau(1)
+        warm(0, 1)
+        xQ(3)
+        st(2, 3)
+        Vs(1)
+        mx(3, 0, 0)
+        mx(3, 2, 3)
+        Ga(2)
+        cp(2, 0)
+        ge(1, 3)
+        ge(1, 2)
+        mx(3, 3, 6)
         ge(0, 1)
         ge(0, 2)
-        ge(0, 3)
-        st(2, 0)
-        Vau(1)
-        xQ(3)
+        st(3, 0)
+        Vb(2)
+        st(3, 2)
+        Vc(2)
+        mmS(2, 1)
         mx(3, 1, 5)
-        mx(3, 0, 4)
-        st(2, 2)
-        Vs(1)
-        st(2, 3)
-        mx(3, 2, 6)
-        ge(1, 3)
+        st(3, 3)
+        Vau(2)
         ge(1, 0)
         ge(1, 1)
-        ge(1, 2)
-        Va(2)
         st(3, 1)
-        Vb(2)
-        st(3, 0)
-        Vc(2)
-        warm(1, 2)
-        mmS(2, 1)
-        mx(3, 3, 7)
-        st(3, 2)
-        Vau(2)
-        st(3, 3)
         Vs(2)
         Va(3)
         ge(2, 1)
-        ge(2, 2)
-        ge(2, 3)
-        ge(2, 0)
         Vb(3)
         Vc(3)
         mmS(3, 1)
+        ge(2, 2)
         Vau(3)
         Vs(3)
+        ge(2, 3)
+        ge(2, 0)
         ge(3, 0)
         ge(3, 1)
         ge(3, 2)

@@ -262,7 +262,7 @@ def tile_axialshift_pa_kernel(tc, x, w1, b1, g1, be1, out):
         wT(1, 5)
         wC(1)
         cvt()
-        warm(1, 4)
+        warm(1, 3)
         xQ(0)
         xR(1, 0, "V")
         xR(1, 1, "S")
@@ -331,7 +331,7 @@ def tile_axialshift_pa_kernel(tc, x, w1, b1, g1, be1, out):
         ge(0, 0)
         st(2, 2)
         Vau(1)
-        warm(0, 1)
+        warm(0, 2)
         xQ(3)
         st(2, 3)
         Vs(1)

from contextlib import ExitStack

import concourse.mybir as mybir
from concourse.masks import make_identity

F32 = mybir.dt.float32
BF16 = mybir.dt.bfloat16
U32 = mybir.dt.uint32
U8 = mybir.dt.uint8
FP8X4 = mybir.dt.float8_e4m3fn_x4
ALU = mybir.AluOpType
ACT = mybir.ActivationFunctionType
AX = mybir.AxisListType

FLOPS = 2 * 1024 * 1024 * 1024

P = 128
NS = 4
NT = 8
NB = 4
PIX = 256
EPS = 1e-5


def tile_axialshift_pa_kernel(tc, x, w1, b1, g1, be1, out):
    nc = tc.nc
    with ExitStack() as ctx:
        keep = ctx.enter_context(tc.tile_pool(name="keep", bufs=1))
        psum = ctx.enter_context(tc.psum_pool(name="psum", bufs=1))
        ctx.enter_context(tc.manual_schedule())

        w_sb = keep.tile([P, NT, 1024], BF16)
        x_sb = keep.tile([P, NS, 2, 4, PIX], BF16)
        wg = keep.tile([P, NT, 2, P, 4], BF16, align_bytes=64)
        xg = keep.tile([P, NS, 2, PIX, 4], BF16, align_bytes=64)
        wc = keep.tile([P, NT, 2 * P], U32, align_bytes=64)
        ws = keep.tile([P, NT, 2 * P], U8, align_bytes=64)
        xc = keep.tile([P, NS, 2 * PIX], U32, align_bytes=64)
        xs = keep.tile([P, NS, 2 * PIX], U8, align_bytes=64)
        o_sb = keep.tile([P, NS, NT, PIX], F32)
        y_sb = keep.tile([P, NS, NT, PIX], F32)

        ident = keep.tile([P, P], F32)
        cmat = keep.tile([P, P], F32)
        brhs = keep.tile([P, 4], F32)
        mhalf = keep.tile([P, 1], F32)
        junk_in = keep.tile([P, 1], F32)
        junk_out = keep.tile([P, 1], F32)
        zeros = keep.tile([P, 512], BF16)
        b_bf = keep.tile([P, NT], BF16)
        g_bf = keep.tile([P, NT], BF16)
        be_bf = keep.tile([P, NT], BF16)
        b32 = keep.tile([P, NT], F32)
        nmb = keep.tile([P, 1], F32)
        addc = keep.tile([P, NT, 2], F32)
        stt = keep.tile([P, NS, NB, 6], F32)
        rr = keep.tile([P, NS, 8], F32)
        gu = keep.tile([P, NS, 2, NT], F32)
        zb = keep.tile([P, 2, NT], F32)
        sb = keep.tile([P, NS, 2, NT], F32)
        ve = [keep.tile([P, 1], F32, name="ve%d" % n) for n in range(NS)]
        rstd = [keep.tile([P, 1], F32, name="rstd%d" % n) for n in range(NS)]

        w_view = w1.rearrange("(p t) k -> p t k", t=NT)
        o_view = [out[n].rearrange("(p t) h w -> p t (h w)", t=NT) for n in range(NS)]
        wt_tiles = {}
        y_tiles = {}
        ps_tiles = {}

        def bank(k, shape, name):
            return psum.tile(shape, F32, tag="bk%d" % k, name=name)

        def params():
            nc.scalar.dma_start(out=b_bf[:], in_=b1.rearrange("(p t) -> p t", t=NT))
            nc.scalar.dma_start(out=g_bf[:], in_=g1.rearrange("(p t) -> p t", t=NT))
            nc.scalar.dma_start(out=be_bf[:], in_=be1.rearrange("(p t) -> p t", t=NT))
            nc.vector.memset(zeros[:], 0.0)
            nc.vector.memset(junk_in[:], 0.0)
            nc.scalar.activation(out=junk_out[:], in_=junk_in[:], func=ACT.Gelu)
            make_identity(nc, ident[:])
            nc.vector.memset(cmat[:], 1.0 / P)
            nc.vector.memset(addc[:], PIX * EPS)
            nc.vector.memset(brhs[:], 0.0)
            nc.vector.memset(mhalf[:], -0.5)
            nc.vector.memset(rr[:], 0.0)
            nc.vector.memset(rr[:, :, 1:2], -1.0)
            nc.vector.memset(zb[:], 0.0)

        def lw(t, m=1):
            nc.sync.dma_start(out=w_sb[:, t:t + m, :], in_=w_view[:, t:t + m, :])

        def lx(n, g):
            nc.sync.dma_start(
                out=x_sb[:, n, g].rearrange("p s w -> p (s w)"),
                in_=x[n, 512 * g:512 * (g + 1)].rearrange("(q s) h w -> q (s h w)", s=4),
            )

        def warm(k, count):
            wm = bank(k, [P, 512], "warm")
            for i in range(count):
                nc.tensor.matmul(wm[:], lhsT=zeros[:, 0:P], rhs=zeros[:], start=True, stop=True)

        def cvt():
            nc.vector.tensor_copy(out=b32[:], in_=b_bf[:])
            nc.vector.tensor_copy(out=gu[:, :, 0, :],
                                  in_=g_bf[:].unsqueeze(1).to_broadcast([P, NS, NT]))
            nc.vector.tensor_copy(out=zb[:, 1, :], in_=be_bf[:])
            nc.vector.tensor_reduce(out=brhs[:, 0:1], in_=b32[:], axis=AX.X, op=ALU.add)

        def mmb(k):
            psb = bank(k, [P, 4], "psb")
            ps_tiles["b"] = psb
            nc.tensor.matmul(psb[:], lhsT=cmat[:], rhs=brhs[:], start=True, stop=True)

        def bp():
            nc.vector.tensor_scalar(out=nmb[:], in0=ps_tiles["b"][:, 0:1], scalar1=-1.0 / NT,
                                    scalar2=None, op0=ALU.mult)
            nc.vector.tensor_scalar(out=addc[:, :, 0], in0=b32[:], scalar1=nmb[:], scalar2=None,
                                    op0=ALU.add)

        def wT(t, k):
            wt = bank(k, [P, 4, P], "wt%d" % t)
            wt_tiles[t] = wt
            words = w_sb[:, t, :].bitcast(F32)
            for a in range(4):
                g, u = divmod(a, 2)
                nc.tensor.transpose(wt[:, a, :], words[:, 256 * g + u:256 * (g + 1):2], ident[:])

        def wC(t, eng="S"):
            dst = wg[:, t].rearrange("p g o s -> p (g o s)").bitcast(F32)
            dst = dst.rearrange("p (g o u) -> p g o u", g=2, u=2)
            src = wt_tiles[t][:].rearrange("p (g u) o -> p g o u", g=2)
            if eng == "S":
                nc.scalar.copy(out=dst, in_=src)
            else:
                nc.vector.tensor_copy(out=dst, in_=src)

        def wQ(t, m=1):
            nc.vector.quantize_mx(
                out=wc[:, t:t + m, :].rearrange("p t c -> p (t c)").bitcast(FP8X4),
                scales=ws[:, t:t + m, :].rearrange("p t c -> p (t c)"),
                in_=wg[:, t:t + m].rearrange("p t g o s -> p (t g o s)"),
            )

        def xR(n, g, eng):
            dst = xg[:, n, g].rearrange("p (c i) s -> p c s i", i=4)
            src = x_sb[:, n, g].rearrange("p s (c i) -> p c s i", i=4)
            if eng == "V":
                nc.vector.tensor_copy(out=dst, in_=src)
            elif eng == "S":
                nc.scalar.copy(out=dst, in_=src)
            else:
                for c in range(0, PIX, 64):
                    nc.gpsimd.tensor_scalar(
                        out=xg[:, n, g, c:c + 64, :],
                        in0=x_sb[:, n, g, :, c:c + 64].rearrange("p s w -> p w s"),
                        scalar1=1.0, scalar2=0.0, op0=ALU.mult, op1=ALU.add)

        def xQ(n):
            nc.vector.quantize_mx(
                out=xc[:, n, :].bitcast(FP8X4),
                scales=xs[:, n, :],
                in_=xg[:, n].rearrange("p g w s -> p (g w s)"),
            )

        def mx(n, b, k):
            yb = bank(k, [P, 2, PIX], "y%d_%d" % (n, b))
            y_tiles[(n, b)] = yb
            for h in range(2):
                t = 2 * b + h
                for g in range(2):
                    nc.tensor.matmul_mx(
                        out=yb[:, h, :],
                        lhsT=wc[:, t, g * P:(g + 1) * P].bitcast(FP8X4),
                        lhsT_scale=ws[:, t, g * P:(g + 1) * P],
                        rhs=xc[:, n, g * PIX:(g + 1) * PIX].bitcast(FP8X4),
                        rhs_scale=xs[:, n, g * PIX:(g + 1) * PIX],
                        start=(g == 0),
                        stop=(g == 1),
                    )

        def st(n, b):
            nc.vector.bn_stats(out=stt[:, n, b, :],
                               in_=y_tiles[(n, b)][:].rearrange("p h w -> p w h"))

        def cp(n, b):
            nc.scalar.copy(out=y_sb[:, n, 2 * b:2 * b + 2, :], in_=y_tiles[(n, b)][:])
            y_tiles[(n, b)] = y_sb[:, n, 2 * b:2 * b + 2, :]

        def Va(n):
            pairs = stt[:, n].rearrange("p b (h s) -> p (b h) s", s=3)[:, :, 1:3]
            nc.vector.tensor_tensor(out=pairs, in0=pairs, in1=addc[:], op=ALU.add)

        def Ga(n):
            pairs = stt[:, n].rearrange("p b (h s) -> p (b h) s", s=3)[:, :, 1:3]
            nc.gpsimd.tensor_tensor(out=pairs, in0=pairs, in1=addc[:], op=ALU.add)

        def Vb(n):
            nc.vector.bn_aggr(out=rr[:, n, 2:4], in_=stt[:, n].rearrange("p b s -> p (b s)"))

        def Vc(n):
            nc.vector.scalar_tensor_tensor(
                out=rr[:, n, 4:6], in0=rr[:, n, 1:3], scalar=rr[:, n, 2:3],
                in1=rr[:, n, 0:4:3], op0=ALU.mult, op1=ALU.add)

        def V123(n):
            Va(n)
            Vb(n)
            Vc(n)

        def mmS(n, k):
            ps = bank(k, [P, 4], "ps%d" % n)
            ps_tiles[n] = ps
            nc.tensor.matmul(ps[:], lhsT=cmat[:], rhs=rr[:, n, 2:6], start=True, stop=True)

        def Vau(n):
            ps = ps_tiles[n]
            nc.vector.tensor_scalar(out=ve[n][:], in0=ps[:, 0:1], scalar1=ps[:, 2:3],
                                    scalar2=ps[:, 3:4], op0=ALU.mult, op1=ALU.add)
            nc.gpsimd.tensor_tensor(out=rstd[n][:], in0=ve[n][:], in1=mhalf[:], op=ALU.pow)
            nc.vector.scalar_tensor_tensor(
                out=gu[:, n, 1, :], in0=addc[:, :, 0], scalar=ps[:, 2:3], in1=gu[:, n, 0, :],
                op0=ALU.add, op1=ALU.mult)

        def Vs(n):
            nc.vector.scalar_tensor_tensor(
                out=sb[:, n].rearrange("p a t -> p (a t)"),
                in0=gu[:, n].rearrange("p a t -> p (a t)"), scalar=rstd[n][:],
                in1=zb[:].rearrange("p a t -> p (a t)"), op0=ALU.mult, op1=ALU.add)

        def ge(n, b, last=False):
            yb = y_tiles[(n, b)]
            for h in range(2):
                t = 2 * b + h
                nc.scalar.activation(out=o_sb[:, n, t, :], in_=yb[:, h, :], func=ACT.Gelu,
                                     scale=sb[:, n, 0, t:t + 1], bias=sb[:, n, 1, t:t + 1])
                if last:
                    nc.sync.dma_start(out=o_view[n][:, t:t + 1, :], in_=o_sb[:, n, t:t + 1, :])
            if not last:
                nc.sync.dma_start(out=o_view[n][:, 2 * b:2 * b + 2, :],
                                  in_=o_sb[:, n, 2 * b:2 * b + 2, :])

        params()
        lx(0, 0)
        lx(0, 1)
        lw(0)
        lw(1)
        lx(1, 0)
        lx(1, 1)
        lw(2, 2)
        lw(4, 2)
        lw(6, 2)
        lx(2, 0)
        lx(2, 1)
        lx(3, 0)
        lx(3, 1)
        warm(7, 3)
        xR(0, 0, "V")
        xR(0, 1, "V")
        wT(0, 4)
        wC(0)
        wT(1, 5)
        wC(1)
        cvt()
        warm(1, 3)
        xQ(0)
        xR(1, 0, "V")
        xR(1, 1, "S")
        wQ(0, 2)
        mmb(7)
        wT(2, 6)
        wC(2)
        wT(3, 3)
        wC(3)
        mx(0, 0, 0)
        bp()
        xQ(1)
        wT(4, 7)
        wC(4)
        wT(5, 5)
        wC(5)
        st(0, 0)
        wQ(2, 2)
        wT(6, 6)
        wC(6)
        wT(7, 3)
        wC(7)
        mx(0, 1, 2)
        mx(1, 0, 1)
        wQ(4, 2)
        mx(1, 1, 4)
        st(0, 1)
        mx(0, 2, 7)
        wQ(6, 2)
        st(1, 0)
        mx(0, 3, 3)
        mx(1, 2, 5)
        mx(1, 3, 6)
        st(0, 2)
        xR(2, 0, "S")
        xR(2, 1, "S")
        cp(0, 0)
        cp(1, 0)
        st(1, 1)
        st(0, 3)
        cp(0, 1)
        cp(0, 2)
        xQ(2)
        Ga(0)
        st(1, 2)
        Vb(0)
        mx(2, 0, 1)
        mx(2, 1, 2)
        st(1, 3)
        Vc(0)
        mmS(0, 0)
        cp(1, 1)
        Ga(1)
        st(2, 0)
        Vau(0)
        Vb(1)
        mx(2, 2, 7)
        xR(3, 0, "S")
        st(2, 1)
        Vc(1)
        mx(2, 3, 4)
        mmS(1, 0)
        xR(3, 1, "S")
        Vs(0)
        ge(0, 3)
        ge(0, 0)
        st(2, 2)
        Vau(1)
        warm(0, 2)
        xQ(3)
        st(2, 3)
        Vs(1)
        mx(3, 0, 0)
        mx(3, 2, 3)
        Ga(2)
        cp(2, 0)
        ge(1, 3)
        ge(1, 2)
        mx(3, 3, 6)
        ge(0, 1)
        ge(0, 2)
        st(3, 0)
        Vb(2)
        st(3, 2)
        Vc(2)
        mmS(2, 1)
        mx(3, 1, 5)
        st(3, 3)
        Vau(2)
        ge(1, 0)
        ge(1, 1)
        st(3, 1)
        Vs(2)
        Va(3)
        ge(2, 1)
        Vb(3)
        Vc(3)
        mmS(3, 1)
        ge(2, 2)
        Vau(3)
        Vs(3)
        ge(2, 3)
        ge(2, 0)
        ge(3, 0)
        ge(3, 1)
        ge(3, 2)
        ge(3, 3)
